import numpy as np
import ml_dtypes


def mxq(x, axis, fmt="e4m3"):
    dtype, down = {"e4m3": (ml_dtypes.float8_e4m3fn, 7), "e5m2": (ml_dtypes.float8_e5m2, 14)}[fmt]
    v = np.moveaxis(np.asarray(x, np.float32).astype(ml_dtypes.bfloat16).astype(np.float64), axis, -1)
    blocks = v.reshape(v.shape[:-1] + (-1, 32))
    amax = np.abs(blocks).max(-1, keepdims=True)
    byte = np.maximum(np.where(amax > 0, np.frexp(amax)[1] - 1 + 127, 0) - down, 1)
    scale = np.exp2(byte - 127.0)
    codes = (blocks / scale).astype(np.float32).astype(dtype).astype(np.float64)
    return np.moveaxis((codes * scale).reshape(v.shape), -1, axis)


WIDE = False


def mx_kscale(k):
    if not WIDE:
        return np.ones(k)
    levels = np.array([10, -10, 5, -5, 0])
    if k % 512:
        return np.exp2(np.random.permutation(np.resize(levels, k // 32))).repeat(32)
    a = np.empty((k // 512, 16))
    for p in range(k // 512):
        a[p, :8] = np.random.permutation(np.resize(levels, 8))
        for g in range(8):
            far = levels[np.abs(levels - a[p, g]) >= 10]
            a[p, g + 8] = far[np.random.randint(len(far))]
    return np.exp2(a.ravel()).repeat(32)


BF16 = ml_dtypes.bfloat16


def bf(x):
    return np.asarray(x, np.float32).astype(BF16)


def f64(x):
    return np.asarray(x).astype(np.float64)


B, S, V, E, M = 512, 16, 4096, 512, 1024


def setup_inputs():
    s, t = mx_kscale(E), mx_kscale(M)
    return {"y2": bf(np.maximum(np.random.standard_normal((B, E)), 0.0) * s),
            "first": bf(np.random.standard_normal((B, M)) * 0.4 * t),
            "w_second": bf(np.random.standard_normal((M, E)) * 1.4 / np.sqrt(E) / s[None, :]),
            "b_second": bf(np.random.standard_normal(M) * 0.3),
            "w_int": bf(np.random.standard_normal((M, E)) * 1.4 / np.sqrt(E) / s[None, :] * t[:, None]),
            "b_int": bf(np.random.standard_normal(M) * 0.3 * t),
            "w_out": bf(np.random.standard_normal((V, M)) / np.sqrt(M) / t[None, :]),
            "b_out": bf(np.random.standard_normal(V) * 0.3)}


def reference(y2, first, w_second, b_second, w_int, b_int, w_out, b_out):
    y2q = mxq(f64(y2), 1, "e4m3")
    second = np.maximum((y2q @ mxq(f64(w_second), 1, "e4m3").T) + f64(b_second), 0.0)
    inter = np.maximum((y2q @ mxq(f64(w_int), 1, "e4m3").T) + f64(b_int), 0.0)
    z = second * f64(first) + inter
    return (mxq(z, 1, "e4m3") @ mxq(f64(w_out), 1, "e4m3").T) + f64(b_out)

@@ -1,0 +1,278 @@
+from contextlib import ExitStack
+
+import concourse.mybir as mybir
+from concourse.masks import make_identity
+
+F32 = mybir.dt.float32
+BF16 = mybir.dt.bfloat16
+U32 = mybir.dt.uint32
+U8 = mybir.dt.uint8
+FP8X4 = mybir.dt.float8_e4m3fn_x4
+RELU = mybir.ActivationFunctionType.Relu
+ADD = mybir.AluOpType.add
+MULT = mybir.AluOpType.mult
+
+P = 128
+PACK = 4
+K_PASS = P * PACK
+B, E, M, V = 512, 512, 1024, 4096
+B_TILES = B // P
+CHUNKS = M // P
+Z_PASSES = M // K_PASS
+V_BLOCK = 512
+V_BLOCKS = V // V_BLOCK
+V_TILES = V_BLOCK // P
+ACC_BANKS = 4
+
+FLOPS = 2 * B * E * M * 2 + 2 * B * M * V
+
+
+def k_to_partitions(nc, psum_t, ident, pieces, grouped, copies):
+    words = grouped.bitcast(F32)
+    for i in range(len(pieces) // 2):
+        bank = psum_t.tile([P, 2, 2, P], F32, tag="bank")
+        for a in range(2):
+            piece = pieces[2 * i + a].bitcast(F32)
+            for u in range(2):
+                nc.tensor.transpose(bank[:, a, u, :], piece[:, u : 2 * P : 2], ident)
+        copies[i % len(copies)](
+            out=words[:, 4 * P * i : 4 * P * (i + 1)].rearrange(
+                "p (a c u) -> p a c u", a=2, u=2
+            ),
+            in_=bank[:].rearrange("p a u c -> p a c u"),
+        )
+
+
+def tile_smcrossbaby_1_pb_kernel(
+    tc, y2, first, w_second, b_second, w_int, b_int, w_out, b_out, out
+):
+    nc = tc.nc
+    with ExitStack() as ctx:
+        const = ctx.enter_context(tc.tile_pool(name="const", bufs=1))
+        raw = ctx.enter_context(tc.tile_pool(name="raw", bufs=8))
+        group = ctx.enter_context(tc.tile_pool(name="group", bufs=3))
+        keep = ctx.enter_context(tc.tile_pool(name="keep", bufs=1))
+        psum_t = ctx.enter_context(tc.psum_pool(name="psum_t", bufs=4))
+        psum_acc = ctx.enter_context(tc.psum_pool(name="psum_acc", bufs=ACC_BANKS))
+        ctx.enter_context(tc.manual_schedule())
+
+        ident = const.tile([P, P], F32)
+        make_identity(nc, ident[:])
+        ident_bf = const.tile([P, P], BF16)
+        make_identity(nc, ident_bf[:])
+        bo_rows = const.tile([P, V_BLOCK], BF16)
+        nc.vector.memset(bo_rows[:], 0.0)
+        bias_rows = const.tile([P, 4 * P], BF16)
+        nc.vector.memset(bias_rows[:], 0.0)
+
+        nc.sync.dma_start(
+            out=bo_rows[0:V_BLOCKS, :], in_=b_out.rearrange("(j n) -> j n", j=V_BLOCKS)
+        )
+        nc.sync.dma_start(out=bias_rows[0:2, :], in_=b_second.rearrange("(g x) -> g x", g=2))
+        nc.sync.dma_start(out=bias_rows[2:4, :], in_=b_int.rearrange("(g x) -> g x", g=2))
+        y2_raw = raw.tile([P, B_TILES, E], BF16, tag="raw")
+        nc.sync.dma_start(out=y2_raw[:], in_=y2.rearrange("(c r) k -> c r k", r=B_TILES))
+        w2_raw = raw.tile([P, 2, 4, E], BF16, tag="raw")
+        nc.sync.dma_start(
+            out=w2_raw[:], in_=w_second.rearrange("(g c t) k -> c g t k", g=2, t=4)
+        )
+        wi_raw = raw.tile([P, 2, 4, E], BF16, tag="raw")
+        nc.sync.dma_start(
+            out=wi_raw[:], in_=w_int.rearrange("(g c t) k -> c g t k", g=2, t=4)
+        )
+        first_raw = raw.tile([P, B_TILES, M], BF16, tag="raw")
+        nc.sync.dma_start(
+            out=first_raw[:], in_=first.rearrange("(c r) m -> c r m", r=B_TILES)
+        )
+        wo_raw = []
+        for j in range(V_BLOCKS):
+            wo_raw.append(raw.tile([P, V_TILES, M], BF16, tag="raw", name="wo_raw%d" % j))
+            nc.sync.dma_start(
+                out=wo_raw[j][:],
+                in_=w_out[j * V_BLOCK : (j + 1) * V_BLOCK, :].rearrange(
+                    "(s c) k -> c s k", s=V_TILES
+                ),
+            )
+
+        both = [nc.scalar.copy, nc.vector.tensor_copy]
+
+        bias_split = const.tile([P, 4, P], F32)
+        nc.vector.tensor_copy(
+            out=bias_split[:], in_=bias_rows[:].rearrange("p (c t) -> p t c", t=4)
+        )
+        bias_t = psum_t.tile([P, 4, P], F32, tag="bank")
+        for t in range(4):
+            nc.tensor.transpose(bias_t[:, t, :], bias_split[:, t, :], ident[:])
+        bias = const.tile([P, 2, CHUNKS], F32)
+        nc.vector.tensor_copy(
+            out=bias[:].rearrange("p w (g t) -> p w g t", t=4),
+            in_=bias_t[:, :, 0:4].rearrange("p t (w g) -> p w g t", w=2),
+        )
+
+        bo = const.tile([P, V], BF16)
+
+        def spread_b_out(pair):
+            spread = psum_acc.tile([P, 2, V_BLOCK], BF16, tag="acc")
+            for i in range(2):
+                j = 2 * pair + i
+                nc.tensor.matmul(
+                    out=spread[:, i, :],
+                    lhsT=ident_bf[:, j : j + 1].to_broadcast([P, P]),
+                    rhs=bo_rows[:],
+                    start=True,
+                    stop=True,
+                )
+            nc.scalar.copy(
+                out=bo[:, 2 * pair * V_BLOCK : 2 * (pair + 1) * V_BLOCK],
+                in_=spread[:].rearrange("p i n -> p (i n)"),
+            )
+
+        y2_c = keep.tile([P, B], U32, align_bytes=64)
+        y2_s = keep.tile([P, B], U8, align_bytes=64)
+        w2_c = keep.tile([P, M], U32, align_bytes=64)
+        w2_s = keep.tile([P, M], U8, align_bytes=64)
+        wi_c = keep.tile([P, M], U32, align_bytes=64)
+        wi_s = keep.tile([P, M], U8, align_bytes=64)
+
+        def quantise(codes, scales, grouped):
+            nc.vector.quantize_mx(out=codes.bitcast(FP8X4), scales=scales, in_=grouped)
+
+        y2_g = group.tile([P, B * PACK], BF16, tag="group", align_bytes=64)
+        w2_g = group.tile([P, 2, M * PACK // 2], BF16, tag="group", align_bytes=64)
+        wi_g = group.tile([P, 2, M * PACK // 2], BF16, tag="group", align_bytes=64)
+        w2_rows = [w2_raw[:, g, t, :] for g in range(2) for t in range(4)]
+        wi_rows = [wi_raw[:, g, t, :] for g in range(2) for t in range(4)]
+        spread_b_out(0)
+        spread_b_out(1)
+        k_to_partitions(
+            nc,
+            psum_t,
+            ident[:],
+            [y2_raw[:, r, :] for r in range(B_TILES)],
+            y2_g[:],
+            [nc.scalar.copy],
+        )
+        quantise(y2_c[:], y2_s[:], y2_g[:])
+        spread_b_out(2)
+        spread_b_out(3)
+        k_to_partitions(nc, psum_t, ident[:], w2_rows[0:4], w2_g[:, 0, :], [nc.scalar.copy])
+        k_to_partitions(nc, psum_t, ident[:], w2_rows[4:8], w2_g[:, 1, :], [nc.scalar.copy])
+        quantise(w2_c[:, 0 : M // 2], w2_s[:, 0 : M // 2], w2_g[:, 0, :])
+        quantise(w2_c[:, M // 2 : M], w2_s[:, M // 2 : M], w2_g[:, 1, :])
+
+        z_c = keep.tile([P, Z_PASSES, B], U32, align_bytes=64)
+        z_s = keep.tile([P, Z_PASSES, B], U8, align_bytes=64)
+        wo_c = keep.tile([P, V_BLOCKS, Z_PASSES, V_BLOCK], U32, align_bytes=64)
+        wo_s = keep.tile([P, V_BLOCKS, Z_PASSES, V_BLOCK], U8, align_bytes=64)
+        wo_g = [None] * V_BLOCKS
+
+        def transpose_block(j):
+            wo_g[j] = group.tile(
+                [P, Z_PASSES * V_BLOCK * PACK], BF16, tag="group", align_bytes=64, name="wo_g%d" % j
+            )
+            k_to_partitions(
+                nc,
+                psum_t,
+                ident[:],
+                [
+                    wo_raw[j][:, s, g * K_PASS : (g + 1) * K_PASS]
+                    for g in range(Z_PASSES)
+                    for s in range(V_TILES)
+                ],
+                wo_g[j][:],
+                [nc.scalar.copy],
+            )
+
+        def quantise_block(j):
+            quantise(
+                wo_c[:, j, :, :].rearrange("p g n -> p (g n)"),
+                wo_s[:, j, :, :].rearrange("p g n -> p (g n)"),
+                wo_g[j][:],
+            )
+
+        def hidden_layer(w_c, w_s, chunk, bias_col, result):
+            cols = slice(chunk * P, (chunk + 1) * P)
+            acc = psum_acc.tile([P, B], F32, tag="acc")
+            nc.tensor.matmul_mx(
+                out=acc[:],
+                lhsT=w_c[:, cols].bitcast(FP8X4),
+                lhsT_scale=w_s[:, cols],
+                rhs=y2_c[:].bitcast(FP8X4),
+                rhs_scale=y2_s[:],
+                start=True,
+                stop=True,
+            )
+            nc.scalar.activation(out=result, in_=acc[:], func=RELU, bias=bias_col)
+
+        with tc.tile_pool(name="hidden", bufs=1) as hidden:
+            second = hidden.tile([P, CHUNKS, B], F32)
+            inter = hidden.tile([P, CHUNKS, B], F32)
+            z_g = hidden.tile([P, Z_PASSES, B * PACK], BF16, align_bytes=64)
+            for chunk in range(ACC_BANKS):
+                hidden_layer(w2_c, w2_s, chunk, bias[:, 0, chunk : chunk + 1], second[:, chunk, :])
+            k_to_partitions(nc, psum_t, ident[:], wi_rows[0:4], wi_g[:, 0, :], both)
+            k_to_partitions(nc, psum_t, ident[:], wi_rows[4:8], wi_g[:, 1, :], both)
+            for chunk in range(ACC_BANKS, CHUNKS):
+                hidden_layer(w2_c, w2_s, chunk, bias[:, 0, chunk : chunk + 1], second[:, chunk, :])
+            quantise(wi_c[:, 0 : M // 2], wi_s[:, 0 : M // 2], wi_g[:, 0, :])
+            quantise(wi_c[:, M // 2 : M], wi_s[:, M // 2 : M], wi_g[:, 1, :])
+            first_t = []
+            for q in range(4):
+                first_t.append(psum_t.tile([P, B], F32, tag="bank", name="first_t%d" % q))
+                for r in range(B_TILES):
+                    nc.tensor.transpose(
+                        first_t[q][:, r * P : (r + 1) * P],
+                        first_raw[:, r, :].bitcast(F32)[
+                            :, (q // 2) * 2 * P + q % 2 : (q // 2 + 1) * 2 * P : 2
+                        ],
+                        ident[:],
+                    )
+            for q in range(4):
+                nc.vector.tensor_tensor(
+                    out=second[:, 2 * q : 2 * q + 2, :],
+                    in0=second[:, 2 * q : 2 * q + 2, :],
+                    in1=first_t[q][:].bitcast(BF16).rearrange("p (n e) -> p e n", e=2),
+                    op=MULT,
+                )
+            for chunk in range(CHUNKS):
+                hidden_layer(wi_c, wi_s, chunk, bias[:, 1, chunk : chunk + 1], inter[:, chunk, :])
+            transpose_block(0)
+            transpose_block(1)
+            for g in range(Z_PASSES):
+                nc.vector.tensor_tensor(
+                    out=z_g[:, g, :].rearrange("p (n t) -> p n t", t=PACK),
+                    in0=second[:, PACK * g : PACK * (g + 1), :].rearrange("p t n -> p n t"),
+                    in1=inter[:, PACK * g : PACK * (g + 1), :].rearrange("p t n -> p n t"),
+                    op=ADD,
+                )
+            quantise_block(0)
+            quantise(
+                z_c[:].rearrange("p g n -> p (g n)"),
+                z_s[:].rearrange("p g n -> p (g n)"),
+                z_g[:].rearrange("p g x -> p (g x)"),
+            )
+
+        out_rows = out.rearrange("(c r) v -> c r v", r=B_TILES)
+        with tc.tile_pool(name="result", bufs=2 * B_TILES) as result:
+            for j in range(V_BLOCKS):
+                if j + 1 < V_BLOCKS:
+                    quantise_block(j + 1)
+                if j + 2 < V_BLOCKS:
+                    transpose_block(j + 2)
+                cols = slice(j * V_BLOCK, (j + 1) * V_BLOCK)
+                for r in range(B_TILES):
+                    rows = slice(r * P, (r + 1) * P)
+                    acc = psum_acc.tile([P, V_BLOCK], F32, tag="acc")
+                    for g in range(Z_PASSES):
+                        nc.tensor.matmul_mx(
+                            out=acc[:],
+                            lhsT=z_c[:, g, rows].bitcast(FP8X4),
+                            lhsT_scale=z_s[:, g, rows],
+                            rhs=wo_c[:, j, g, :].bitcast(FP8X4),
+                            rhs_scale=wo_s[:, j, g, :],
+                            start=(g == 0),
+                            stop=(g == Z_PASSES - 1),
+                        )
+                    res = result.tile([P, V_BLOCK], F32)
+                    nc.vector.tensor_tensor(out=res[:], in0=acc[:], in1=bo[:, cols], op=ADD)
+                    nc.sync.dma_start(out=out_rows[:, r, cols], in_=res[:])

@@ -18,29 +18,13 @@ K_PASS = P * PACK
 B, E, M, V = 512, 512, 1024, 4096
 B_TILES = B // P
 CHUNKS = M // P
+HALF = CHUNKS // 2
 Z_PASSES = M // K_PASS
 V_BLOCK = 512
 V_BLOCKS = V // V_BLOCK
 V_TILES = V_BLOCK // P
-ACC_BANKS = 4
 
 FLOPS = 2 * B * E * M * 2 + 2 * B * M * V
-
-
-def k_to_partitions(nc, psum_t, ident, pieces, grouped, copies):
-    words = grouped.bitcast(F32)
-    for i in range(len(pieces) // 2):
-        bank = psum_t.tile([P, 2, 2, P], F32, tag="bank")
-        for a in range(2):
-            piece = pieces[2 * i + a].bitcast(F32)
-            for u in range(2):
-                nc.tensor.transpose(bank[:, a, u, :], piece[:, u : 2 * P : 2], ident)
-        copies[i % len(copies)](
-            out=words[:, 4 * P * i : 4 * P * (i + 1)].rearrange(
-                "p (a c u) -> p a c u", a=2, u=2
-            ),
-            in_=bank[:].rearrange("p a u c -> p a c u"),
-        )
 
 
 def tile_smcrossbaby_1_pb_kernel(
@@ -49,44 +33,47 @@ def tile_smcrossbaby_1_pb_kernel(
     nc = tc.nc
     with ExitStack() as ctx:
         const = ctx.enter_context(tc.tile_pool(name="const", bufs=1))
-        raw = ctx.enter_context(tc.tile_pool(name="raw", bufs=8))
+        raw = ctx.enter_context(tc.tile_pool(name="raw", bufs=1))
+        stream = ctx.enter_context(tc.tile_pool(name="stream", bufs=6))
         group = ctx.enter_context(tc.tile_pool(name="group", bufs=3))
+        codes = ctx.enter_context(tc.tile_pool(name="codes", bufs=3))
         keep = ctx.enter_context(tc.tile_pool(name="keep", bufs=1))
+        result = ctx.enter_context(tc.tile_pool(name="result", bufs=8))
         psum_t = ctx.enter_context(tc.psum_pool(name="psum_t", bufs=4))
-        psum_acc = ctx.enter_context(tc.psum_pool(name="psum_acc", bufs=ACC_BANKS))
+        psum_acc = ctx.enter_context(tc.psum_pool(name="psum_acc", bufs=4))
         ctx.enter_context(tc.manual_schedule())
 
         ident = const.tile([P, P], F32)
         make_identity(nc, ident[:])
-        ident_bf = const.tile([P, P], BF16)
-        make_identity(nc, ident_bf[:])
-        bo_rows = const.tile([P, V_BLOCK], BF16)
-        nc.vector.memset(bo_rows[:], 0.0)
-        bias_rows = const.tile([P, 4 * P], BF16)
-        nc.vector.memset(bias_rows[:], 0.0)
 
-        nc.sync.dma_start(
-            out=bo_rows[0:V_BLOCKS, :], in_=b_out.rearrange("(j n) -> j n", j=V_BLOCKS)
-        )
-        nc.sync.dma_start(out=bias_rows[0:2, :], in_=b_second.rearrange("(g x) -> g x", g=2))
-        nc.sync.dma_start(out=bias_rows[2:4, :], in_=b_int.rearrange("(g x) -> g x", g=2))
-        y2_raw = raw.tile([P, B_TILES, E], BF16, tag="raw")
-        nc.sync.dma_start(out=y2_raw[:], in_=y2.rearrange("(c r) k -> c r k", r=B_TILES))
-        w2_raw = raw.tile([P, 2, 4, E], BF16, tag="raw")
-        nc.sync.dma_start(
-            out=w2_raw[:], in_=w_second.rearrange("(g c t) k -> c g t k", g=2, t=4)
-        )
-        wi_raw = raw.tile([P, 2, 4, E], BF16, tag="raw")
-        nc.sync.dma_start(
-            out=wi_raw[:], in_=w_int.rearrange("(g c t) k -> c g t k", g=2, t=4)
-        )
-        first_raw = raw.tile([P, B_TILES, M], BF16, tag="raw")
+        y2_raw = raw.tile([P, B_TILES, E], BF16)
+        w2_raw = raw.tile([P, Z_PASSES, PACK, E], BF16)
+        wi_raw = raw.tile([P, Z_PASSES, PACK, E], BF16)
+        first_raw = raw.tile([P, B_TILES, M], BF16)
+        b2 = const.tile([P, Z_PASSES, PACK], BF16)
+        bi = const.tile([P, Z_PASSES, PACK], BF16)
+        bo = const.tile([P, V], BF16)
+
+        y2_rows = y2.rearrange("(c r) k -> c r k", r=B_TILES)
+        w2_rows = w_second.rearrange("(g c t) k -> c g t k", g=Z_PASSES, t=PACK)
+        wi_rows = w_int.rearrange("(g c t) k -> c g t k", g=Z_PASSES, t=PACK)
+        nc.sync.dma_start(out=y2_raw[:, 0:2, :], in_=y2_rows[:, 0:2, :])
+        nc.sync.dma_start(out=y2_raw[:, 2:4, :], in_=y2_rows[:, 2:4, :])
+        for g in range(Z_PASSES):
+            nc.sync.dma_start(out=w2_raw[:, g, :, :], in_=w2_rows[:, g, :, :])
+        for bias, vector in ((b2, b_second), (bi, b_int)):
+            nc.sync.dma_start(
+                out=bias[:], in_=vector.rearrange("(g c t) -> c g t", g=Z_PASSES, t=PACK)
+            )
+        for g in range(Z_PASSES):
+            nc.sync.dma_start(out=wi_raw[:, g, :, :], in_=wi_rows[:, g, :, :])
         nc.sync.dma_start(
             out=first_raw[:], in_=first.rearrange("(c r) m -> c r m", r=B_TILES)
         )
         wo_raw = []
-        for j in range(V_BLOCKS):
-            wo_raw.append(raw.tile([P, V_TILES, M], BF16, tag="raw", name="wo_raw%d" % j))
+
+        def load_block(j):
+            wo_raw.append(stream.tile([P, V_TILES, M], BF16, tag="wo_raw", name="wo_raw%d" % j))
             nc.sync.dma_start(
                 out=wo_raw[j][:],
                 in_=w_out[j * V_BLOCK : (j + 1) * V_BLOCK, :].rearrange(
@@ -94,103 +81,65 @@ def tile_smcrossbaby_1_pb_kernel(
                 ),
             )
 
-        both = [nc.scalar.copy, nc.vector.tensor_copy]
+        for j in range(3):
+            load_block(j)
+        nc.sync.dma_start(out=bo[:], in_=b_out.partition_broadcast(P))
+        for j in range(3, V_BLOCKS):
+            load_block(j)
 
-        bias_split = const.tile([P, 4, P], F32)
-        nc.vector.tensor_copy(
-            out=bias_split[:], in_=bias_rows[:].rearrange("p (c t) -> p t c", t=4)
-        )
-        bias_t = psum_t.tile([P, 4, P], F32, tag="bank")
-        for t in range(4):
-            nc.tensor.transpose(bias_t[:, t, :], bias_split[:, t, :], ident[:])
-        bias = const.tile([P, 2, CHUNKS], F32)
-        nc.vector.tensor_copy(
-            out=bias[:].rearrange("p w (g t) -> p w g t", t=4),
-            in_=bias_t[:, :, 0:4].rearrange("p t (w g) -> p w g t", w=2),
-        )
+        on_scalar, on_vector = nc.scalar.copy, nc.vector.tensor_copy
 
-        bo = const.tile([P, V], BF16)
-
-        def spread_b_out(pair):
-            spread = psum_acc.tile([P, 2, V_BLOCK], BF16, tag="acc")
-            for i in range(2):
-                j = 2 * pair + i
-                nc.tensor.matmul(
-                    out=spread[:, i, :],
-                    lhsT=ident_bf[:, j : j + 1].to_broadcast([P, P]),
-                    rhs=bo_rows[:],
-                    start=True,
-                    stop=True,
-                )
-            nc.scalar.copy(
-                out=bo[:, 2 * pair * V_BLOCK : 2 * (pair + 1) * V_BLOCK],
-                in_=spread[:].rearrange("p i n -> p (i n)"),
+        def turn(pieces, grouped, copy):
+            bank = psum_t.tile([P, 2, 2, P], F32, tag="bank")
+            for a in range(2):
+                words = pieces[a].bitcast(F32)
+                for u in range(2):
+                    nc.tensor.transpose(bank[:, a, u, :], words[:, u : 2 * P : 2], ident[:])
+            copy(
+                out=grouped.bitcast(F32).rearrange("p (a c u) -> p a c u", a=2, u=2),
+                in_=bank[:].rearrange("p a u c -> p a c u"),
             )
 
+        TURN = 2 * P * PACK
+
+        def quantise(codes_, scales, grouped):
+            nc.vector.quantize_mx(out=codes_.bitcast(FP8X4), scales=scales, in_=grouped)
+
+        y2_g = keep.tile([P, B * PACK], BF16, align_bytes=64)
+        w2_g = keep.tile([P, Z_PASSES, M * PACK // 2], BF16, align_bytes=64)
+        wi_g = keep.tile([P, Z_PASSES, M * PACK // 2], BF16, align_bytes=64)
+        z_g = keep.tile([P, Z_PASSES, B * PACK], BF16, align_bytes=64)
         y2_c = keep.tile([P, B], U32, align_bytes=64)
         y2_s = keep.tile([P, B], U8, align_bytes=64)
         w2_c = keep.tile([P, M], U32, align_bytes=64)
         w2_s = keep.tile([P, M], U8, align_bytes=64)
         wi_c = keep.tile([P, M], U32, align_bytes=64)
         wi_s = keep.tile([P, M], U8, align_bytes=64)
-
-        def quantise(codes, scales, grouped):
-            nc.vector.quantize_mx(out=codes.bitcast(FP8X4), scales=scales, in_=grouped)
-
-        y2_g = group.tile([P, B * PACK], BF16, tag="group", align_bytes=64)
-        w2_g = group.tile([P, 2, M * PACK // 2], BF16, tag="group", align_bytes=64)
-        wi_g = group.tile([P, 2, M * PACK // 2], BF16, tag="group", align_bytes=64)
-        w2_rows = [w2_raw[:, g, t, :] for g in range(2) for t in range(4)]
-        wi_rows = [wi_raw[:, g, t, :] for g in range(2) for t in range(4)]
-        spread_b_out(0)
-        spread_b_out(1)
-        k_to_partitions(
-            nc,
-            psum_t,
-            ident[:],
-            [y2_raw[:, r, :] for r in range(B_TILES)],
-            y2_g[:],
-            [nc.scalar.copy],
-        )
-        quantise(y2_c[:], y2_s[:], y2_g[:])
-        spread_b_out(2)
-        spread_b_out(3)
-        k_to_partitions(nc, psum_t, ident[:], w2_rows[0:4], w2_g[:, 0, :], [nc.scalar.copy])
-        k_to_partitions(nc, psum_t, ident[:], w2_rows[4:8], w2_g[:, 1, :], [nc.scalar.copy])
-        quantise(w2_c[:, 0 : M // 2], w2_s[:, 0 : M // 2], w2_g[:, 0, :])
-        quantise(w2_c[:, M // 2 : M], w2_s[:, M // 2 : M], w2_g[:, 1, :])
-
         z_c = keep.tile([P, Z_PASSES, B], U32, align_bytes=64)
         z_s = keep.tile([P, Z_PASSES, B], U8, align_bytes=64)
-        wo_c = keep.tile([P, V_BLOCKS, Z_PASSES, V_BLOCK], U32, align_bytes=64)
-        wo_s = keep.tile([P, V_BLOCKS, Z_PASSES, V_BLOCK], U8, align_bytes=64)
-        wo_g = [None] * V_BLOCKS
+        second = keep.tile([P, CHUNKS, B], F32)
+        inter = keep.tile([P, CHUNKS, B], F32)
 
-        def transpose_block(j):
-            wo_g[j] = group.tile(
-                [P, Z_PASSES * V_BLOCK * PACK], BF16, tag="group", align_bytes=64, name="wo_g%d" % j
-            )
-            k_to_partitions(
-                nc,
-                psum_t,
-                ident[:],
-                [
-                    wo_raw[j][:, s, g * K_PASS : (g + 1) * K_PASS]
-                    for g in range(Z_PASSES)
-                    for s in range(V_TILES)
-                ],
-                wo_g[j][:],
-                [nc.scalar.copy],
+        def turn_y2(i, copy):
+            turn(
+                [y2_raw[:, 2 * i, :], y2_raw[:, 2 * i + 1, :]],
+                y2_g[:, i * TURN : (i + 1) * TURN],
+                copy,
             )
 
-        def quantise_block(j):
-            quantise(
-                wo_c[:, j, :, :].rearrange("p g n -> p (g n)"),
-                wo_s[:, j, :, :].rearrange("p g n -> p (g n)"),
-                wo_g[j][:],
+        def turn_weight(w_raw, w_g, i, copy):
+            g, h = i // 2, i % 2
+            turn(
+                [w_raw[:, g, 2 * h, :], w_raw[:, g, 2 * h + 1, :]],
+                w_g[:, g, h * TURN : (h + 1) * TURN],
+                copy,
             )
 
-        def hidden_layer(w_c, w_s, chunk, bias_col, result):
+        def quantise_weight(w_g, w_c, w_s, g):
+            cols = slice(g * M // 2, (g + 1) * M // 2)
+            quantise(w_c[:, cols], w_s[:, cols], w_g[:, g, :])
+
+        def hidden_layer(w_c, w_s, bias, chunk, dest):
             cols = slice(chunk * P, (chunk + 1) * P)
             acc = psum_acc.tile([P, B], F32, tag="acc")
             nc.tensor.matmul_mx(
@@ -202,77 +151,144 @@ def tile_smcrossbaby_1_pb_kernel(
                 start=True,
                 stop=True,
             )
-            nc.scalar.activation(out=result, in_=acc[:], func=RELU, bias=bias_col)
+            g, t = chunk // PACK, chunk % PACK
+            nc.scalar.activation(
+                out=dest[:, chunk, :], in_=acc[:], func=RELU, bias=bias[:, g, t : t + 1]
+            )
 
-        with tc.tile_pool(name="hidden", bufs=1) as hidden:
-            second = hidden.tile([P, CHUNKS, B], F32)
-            inter = hidden.tile([P, CHUNKS, B], F32)
-            z_g = hidden.tile([P, Z_PASSES, B * PACK], BF16, align_bytes=64)
-            for chunk in range(ACC_BANKS):
-                hidden_layer(w2_c, w2_s, chunk, bias[:, 0, chunk : chunk + 1], second[:, chunk, :])
-            k_to_partitions(nc, psum_t, ident[:], wi_rows[0:4], wi_g[:, 0, :], both)
-            k_to_partitions(nc, psum_t, ident[:], wi_rows[4:8], wi_g[:, 1, :], both)
-            for chunk in range(ACC_BANKS, CHUNKS):
-                hidden_layer(w2_c, w2_s, chunk, bias[:, 0, chunk : chunk + 1], second[:, chunk, :])
-            quantise(wi_c[:, 0 : M // 2], wi_s[:, 0 : M // 2], wi_g[:, 0, :])
-            quantise(wi_c[:, M // 2 : M], wi_s[:, M // 2 : M], wi_g[:, 1, :])
-            first_t = []
-            for q in range(4):
-                first_t.append(psum_t.tile([P, B], F32, tag="bank", name="first_t%d" % q))
-                for r in range(B_TILES):
-                    nc.tensor.transpose(
-                        first_t[q][:, r * P : (r + 1) * P],
-                        first_raw[:, r, :].bitcast(F32)[
-                            :, (q // 2) * 2 * P + q % 2 : (q // 2 + 1) * 2 * P : 2
-                        ],
-                        ident[:],
+        def times_first(q):
+            g, u = q // 2, q % 2
+            first_t = psum_t.tile([P, B], F32, tag="bank")
+            for r in range(B_TILES):
+                nc.tensor.transpose(
+                    first_t[:, r * P : (r + 1) * P],
+                    first_raw[:, r, :].bitcast(F32)[:, 2 * P * g + u : 2 * P * (g + 1) : 2],
+                    ident[:],
+                )
+            nc.vector.tensor_tensor(
+                out=second[:, 2 * q : 2 * q + 2, :],
+                in0=second[:, 2 * q : 2 * q + 2, :],
+                in1=first_t[:].bitcast(BF16).rearrange("p (n e) -> p e n", e=2),
+                op=MULT,
+            )
+
+        def add_inter(g):
+            nc.vector.tensor_tensor(
+                out=z_g[:, g, :].rearrange("p (n t) -> p n t", t=PACK),
+                in0=second[:, PACK * g : PACK * (g + 1), :].rearrange("p t n -> p n t"),
+                in1=inter[:, PACK * g : PACK * (g + 1), :].rearrange("p t n -> p n t"),
+                op=ADD,
+            )
+
+        wo_g, wo_c, wo_s = [], [], []
+
+        def turn_block(j, i, copy):
+            if i == 0:
+                wo_g.append(
+                    group.tile(
+                        [P, Z_PASSES, V_BLOCK * PACK],
+                        BF16,
+                        tag="wo_g",
+                        align_bytes=64,
+                        name="wo_g%d" % j,
                     )
-            for q in range(4):
-                nc.vector.tensor_tensor(
-                    out=second[:, 2 * q : 2 * q + 2, :],
-                    in0=second[:, 2 * q : 2 * q + 2, :],
-                    in1=first_t[q][:].bitcast(BF16).rearrange("p (n e) -> p e n", e=2),
-                    op=MULT,
                 )
-            for chunk in range(CHUNKS):
-                hidden_layer(wi_c, wi_s, chunk, bias[:, 1, chunk : chunk + 1], inter[:, chunk, :])
-            transpose_block(0)
-            transpose_block(1)
-            for g in range(Z_PASSES):
-                nc.vector.tensor_tensor(
-                    out=z_g[:, g, :].rearrange("p (n t) -> p n t", t=PACK),
-                    in0=second[:, PACK * g : PACK * (g + 1), :].rearrange("p t n -> p n t"),
-                    in1=inter[:, PACK * g : PACK * (g + 1), :].rearrange("p t n -> p n t"),
-                    op=ADD,
+            g, h = i // 2, i % 2
+            cols = slice(g * K_PASS, (g + 1) * K_PASS)
+            turn(
+                [wo_raw[j][:, 2 * h, cols], wo_raw[j][:, 2 * h + 1, cols]],
+                wo_g[j][:, g, h * TURN : (h + 1) * TURN],
+                copy,
+            )
+
+        def quantise_block(j):
+            wo_c.append(
+                codes.tile(
+                    [P, Z_PASSES, V_BLOCK], U32, tag="wo_c", align_bytes=64, name="wo_c%d" % j
                 )
-            quantise_block(0)
+            )
+            wo_s.append(
+                codes.tile(
+                    [P, Z_PASSES, V_BLOCK], U8, tag="wo_s", align_bytes=64, name="wo_s%d" % j
+                )
+            )
             quantise(
-                z_c[:].rearrange("p g n -> p (g n)"),
-                z_s[:].rearrange("p g n -> p (g n)"),
-                z_g[:].rearrange("p g x -> p (g x)"),
+                wo_c[j][:].rearrange("p g n -> p (g n)"),
+                wo_s[j][:].rearrange("p g n -> p (g n)"),
+                wo_g[j][:].rearrange("p g x -> p (g x)"),
             )
 
         out_rows = out.rearrange("(c r) v -> c r v", r=B_TILES)
-        with tc.tile_pool(name="result", bufs=2 * B_TILES) as result:
-            for j in range(V_BLOCKS):
-                if j + 1 < V_BLOCKS:
-                    quantise_block(j + 1)
-                if j + 2 < V_BLOCKS:
-                    transpose_block(j + 2)
-                cols = slice(j * V_BLOCK, (j + 1) * V_BLOCK)
-                for r in range(B_TILES):
-                    rows = slice(r * P, (r + 1) * P)
-                    acc = psum_acc.tile([P, V_BLOCK], F32, tag="acc")
-                    for g in range(Z_PASSES):
-                        nc.tensor.matmul_mx(
-                            out=acc[:],
-                            lhsT=z_c[:, g, rows].bitcast(FP8X4),
-                            lhsT_scale=z_s[:, g, rows],
-                            rhs=wo_c[:, j, g, :].bitcast(FP8X4),
-                            rhs_scale=wo_s[:, j, g, :],
-                            start=(g == 0),
-                            stop=(g == Z_PASSES - 1),
-                        )
-                    res = result.tile([P, V_BLOCK], F32)
-                    nc.vector.tensor_tensor(out=res[:], in0=acc[:], in1=bo[:, cols], op=ADD)
-                    nc.sync.dma_start(out=out_rows[:, r, cols], in_=res[:])
+
+        def output_tile(j, r):
+            cols = slice(j * V_BLOCK, (j + 1) * V_BLOCK)
+            rows = slice(r * P, (r + 1) * P)
+            acc = psum_acc.tile([P, V_BLOCK], F32, tag="acc")
+            for g in range(Z_PASSES):
+                nc.tensor.matmul_mx(
+                    out=acc[:],
+                    lhsT=z_c[:, g, rows].bitcast(FP8X4),
+                    lhsT_scale=z_s[:, g, rows],
+                    rhs=wo_c[j][:, g, :].bitcast(FP8X4),
+                    rhs_scale=wo_s[j][:, g, :],
+                    start=(g == 0),
+                    stop=(g == Z_PASSES - 1),
+                )
+            res = result.tile([P, V_BLOCK], F32)
+            nc.vector.tensor_tensor(out=res[:], in0=acc[:], in1=bo[:, cols], op=ADD)
+            nc.sync.dma_start(out=out_rows[:, r, cols], in_=res[:])
+
+        turn_y2(0, on_scalar)
+        turn_y2(1, on_vector)
+        quantise(y2_c[:], y2_s[:], y2_g[:])
+        turn_weight(w2_raw, w2_g, 0, on_scalar)
+        turn_weight(w2_raw, w2_g, 1, on_vector)
+        turn_weight(w2_raw, w2_g, 2, on_scalar)
+        turn_weight(w2_raw, w2_g, 3, on_scalar)
+        quantise_weight(w2_g, w2_c, w2_s, 0)
+        quantise_weight(w2_g, w2_c, w2_s, 1)
+        turn_weight(wi_raw, wi_g, 0, on_scalar)
+        turn_weight(wi_raw, wi_g, 1, on_vector)
+        for chunk in range(4):
+            hidden_layer(w2_c, w2_s, b2, chunk, second)
+        turn_weight(wi_raw, wi_g, 2, on_scalar)
+        turn_weight(wi_raw, wi_g, 3, on_vector)
+        quantise_weight(wi_g, wi_c, wi_s, 0)
+        for chunk in range(4, 8):
+            hidden_layer(w2_c, w2_s, b2, chunk, second)
+        quantise_weight(wi_g, wi_c, wi_s, 1)
+        times_first(0)
+        times_first(1)
+        for chunk in range(4):
+            hidden_layer(wi_c, wi_s, bi, chunk, inter)
+        times_first(2)
+        times_first(3)
+        for chunk in range(4, 8):
+            hidden_layer(wi_c, wi_s, bi, chunk, inter)
+        turn_block(0, 0, on_scalar)
+        turn_block(0, 1, on_scalar)
+        turn_block(0, 2, on_scalar)
+        turn_block(0, 3, on_scalar)
+        add_inter(0)
+        quantise_block(0)
+        add_inter(1)
+        quantise(z_c[:, 0, :], z_s[:, 0, :], z_g[:, 0, :])
+        turn_block(1, 0, on_scalar)
+        turn_block(1, 1, on_scalar)
+        turn_block(1, 2, on_scalar)
+        turn_block(1, 3, on_scalar)
+        quantise(z_c[:, 1, :], z_s[:, 1, :], z_g[:, 1, :])
+        quantise_block(1)
+        turn_block(2, 0, on_scalar)
+        turn_block(2, 1, on_scalar)
+        turn_block(2, 2, on_scalar)
+        turn_block(2, 3, on_scalar)
+
+        for j in range(V_BLOCKS):
+            for r in range(B_TILES):
+                output_tile(j, r)
+            if j + 2 < V_BLOCKS:
+                quantise_block(j + 2)
+            if j + 3 < V_BLOCKS:
+                for i in range(4):
+                    turn_block(j + 3, i, on_scalar)

@@ -34,7 +34,8 @@ def tile_smcrossbaby_1_pb_kernel(
     with ExitStack() as ctx:
         const = ctx.enter_context(tc.tile_pool(name="const", bufs=1))
         raw = ctx.enter_context(tc.tile_pool(name="raw", bufs=1))
-        stream = ctx.enter_context(tc.tile_pool(name="stream", bufs=6))
+        stream = ctx.enter_context(tc.tile_pool(name="stream", bufs=5))
+        sorted_ = ctx.enter_context(tc.tile_pool(name="sorted", bufs=2))
         group = ctx.enter_context(tc.tile_pool(name="group", bufs=3))
         codes = ctx.enter_context(tc.tile_pool(name="codes", bufs=3))
         keep = ctx.enter_context(tc.tile_pool(name="keep", bufs=1))
@@ -89,12 +90,13 @@ def tile_smcrossbaby_1_pb_kernel(
 
         on_scalar, on_vector = nc.scalar.copy, nc.vector.tensor_copy
 
-        def turn(pieces, grouped, copy):
+        def turn(pieces, grouped, copy, sorted_words=False):
             bank = psum_t.tile([P, 2, 2, P], F32, tag="bank")
             for a in range(2):
                 words = pieces[a].bitcast(F32)
                 for u in range(2):
-                    nc.tensor.transpose(bank[:, a, u, :], words[:, u : 2 * P : 2], ident[:])
+                    block = words[:, u * P : (u + 1) * P] if sorted_words else words[:, u : 2 * P : 2]
+                    nc.tensor.transpose(bank[:, a, u, :], block, ident[:])
             copy(
                 out=grouped.bitcast(F32).rearrange("p (a c u) -> p a c u", a=2, u=2),
                 in_=bank[:].rearrange("p a u c -> p a c u"),
@@ -181,6 +183,17 @@ def tile_smcrossbaby_1_pb_kernel(
             )
 
         wo_g, wo_c, wo_s = [], [], []
+        wo_sorted = {}
+
+        def sort_words(j, s, copy):
+            if s == 0:
+                wo_sorted[j] = sorted_.tile(
+                    [P, V_TILES, M], BF16, tag="wo_sorted", name="wo_sorted%d" % j
+                )
+            copy(
+                out=wo_sorted[j][:, s, :].bitcast(F32).rearrange("p (g u w) -> p g u w", g=2, u=2),
+                in_=wo_raw[j][:, s, :].bitcast(F32).rearrange("p (g w u) -> p g u w", g=2, u=2),
+            )
 
         def turn_block(j, i, copy):
             if i == 0:
@@ -195,10 +208,12 @@ def tile_smcrossbaby_1_pb_kernel(
                 )
             g, h = i // 2, i % 2
             cols = slice(g * K_PASS, (g + 1) * K_PASS)
+            source = wo_sorted.get(j, wo_raw[j])
             turn(
-                [wo_raw[j][:, 2 * h, cols], wo_raw[j][:, 2 * h + 1, cols]],
+                [source[:, 2 * h, cols], source[:, 2 * h + 1, cols]],
                 wo_g[j][:, g, h * TURN : (h + 1) * TURN],
                 copy,
+                j in wo_sorted,
             )
 
         def quantise_block(j):
@@ -247,11 +262,11 @@ def tile_smcrossbaby_1_pb_kernel(
         turn_weight(w2_raw, w2_g, 3, on_scalar)
         quantise_weight(w2_g, w2_c, w2_s, 0)
         quantise_weight(w2_g, w2_c, w2_s, 1)
-        turn_weight(wi_raw, wi_g, 0, on_scalar)
-        turn_weight(wi_raw, wi_g, 1, on_vector)
-        for chunk in range(4):
+        turn_weight(wi_raw, wi_g, 0, on_vector)
+        turn_weight(wi_raw, wi_g, 1, on_scalar)
+        for chunk in range(0, 4):
             hidden_layer(w2_c, w2_s, b2, chunk, second)
-        turn_weight(wi_raw, wi_g, 2, on_scalar)
+        turn_weight(wi_raw, wi_g, 2, on_vector)
         turn_weight(wi_raw, wi_g, 3, on_vector)
         quantise_weight(wi_g, wi_c, wi_s, 0)
         for chunk in range(4, 8):
@@ -259,36 +274,79 @@ def tile_smcrossbaby_1_pb_kernel(
         quantise_weight(wi_g, wi_c, wi_s, 1)
         times_first(0)
         times_first(1)
-        for chunk in range(4):
+        for chunk in range(0, 4):
             hidden_layer(wi_c, wi_s, bi, chunk, inter)
         times_first(2)
         times_first(3)
         for chunk in range(4, 8):
             hidden_layer(wi_c, wi_s, bi, chunk, inter)
+        add_inter(0)
         turn_block(0, 0, on_scalar)
         turn_block(0, 1, on_scalar)
         turn_block(0, 2, on_scalar)
         turn_block(0, 3, on_scalar)
-        add_inter(0)
-        quantise_block(0)
         add_inter(1)
         quantise(z_c[:, 0, :], z_s[:, 0, :], z_g[:, 0, :])
+        quantise_block(0)
+        quantise(z_c[:, 1, :], z_s[:, 1, :], z_g[:, 1, :])
         turn_block(1, 0, on_scalar)
         turn_block(1, 1, on_scalar)
         turn_block(1, 2, on_scalar)
         turn_block(1, 3, on_scalar)
-        quantise(z_c[:, 1, :], z_s[:, 1, :], z_g[:, 1, :])
         quantise_block(1)
         turn_block(2, 0, on_scalar)
         turn_block(2, 1, on_scalar)
         turn_block(2, 2, on_scalar)
         turn_block(2, 3, on_scalar)
-
-        for j in range(V_BLOCKS):
-            for r in range(B_TILES):
-                output_tile(j, r)
-            if j + 2 < V_BLOCKS:
-                quantise_block(j + 2)
-            if j + 3 < V_BLOCKS:
-                for i in range(4):
-                    turn_block(j + 3, i, on_scalar)
+        for s in range(V_TILES):
+            sort_words(3, s, on_scalar)
+        for r in range(B_TILES):
+            output_tile(0, r)
+        quantise_block(2)
+        turn_block(3, 0, on_scalar)
+        turn_block(3, 1, on_scalar)
+        turn_block(3, 2, on_scalar)
+        turn_block(3, 3, on_vector)
+        for s in range(V_TILES):
+            sort_words(4, s, on_scalar)
+        for r in range(B_TILES):
+            output_tile(1, r)
+        quantise_block(3)
+        turn_block(4, 0, on_scalar)
+        turn_block(4, 1, on_scalar)
+        turn_block(4, 2, on_scalar)
+        turn_block(4, 3, on_vector)
+        for s in range(V_TILES):
+            sort_words(5, s, on_scalar)
+        for r in range(B_TILES):
+            output_tile(2, r)
+        quantise_block(4)
+        turn_block(5, 0, on_scalar)
+        turn_block(5, 1, on_scalar)
+        turn_block(5, 2, on_scalar)
+        turn_block(5, 3, on_vector)
+        for s in range(V_TILES):
+            sort_words(6, s, on_scalar)
+        for r in range(B_TILES):
+            output_tile(3, r)
+        quantise_block(5)
+        turn_block(6, 0, on_scalar)
+        turn_block(6, 1, on_scalar)
+        turn_block(6, 2, on_scalar)
+        turn_block(6, 3, on_vector)
+        for s in range(V_TILES):
+            sort_words(7, s, on_scalar)
+        for r in range(B_TILES):
+            output_tile(4, r)
+        quantise_block(6)
+        turn_block(7, 0, on_scalar)
+        turn_block(7, 1, on_scalar)
+        turn_block(7, 2, on_scalar)
+        turn_block(7, 3, on_vector)
+        for r in range(B_TILES):
+            output_tile(5, r)
+        quantise_block(7)
+        for r in range(B_TILES):
+            output_tile(6, r)
+        for r in range(B_TILES):
+            output_tile(7, r)

from contextlib import ExitStack

import concourse.mybir as mybir
from concourse.masks import make_identity

F32 = mybir.dt.float32
BF16 = mybir.dt.bfloat16
U32 = mybir.dt.uint32
U8 = mybir.dt.uint8
FP8X4 = mybir.dt.float8_e4m3fn_x4
RELU = mybir.ActivationFunctionType.Relu
ADD = mybir.AluOpType.add
MULT = mybir.AluOpType.mult

P = 128
PACK = 4
K_PASS = P * PACK
B, E, M, V = 512, 512, 1024, 4096
B_TILES = B // P
CHUNKS = M // P
HALF = CHUNKS // 2
Z_PASSES = M // K_PASS
V_BLOCK = 512
V_BLOCKS = V // V_BLOCK
V_TILES = V_BLOCK // P

FLOPS = 2 * B * E * M * 2 + 2 * B * M * V


def tile_smcrossbaby_1_pb_kernel(
    tc, y2, first, w_second, b_second, w_int, b_int, w_out, b_out, out
):
    nc = tc.nc
    with ExitStack() as ctx:
        const = ctx.enter_context(tc.tile_pool(name="const", bufs=1))
        raw = ctx.enter_context(tc.tile_pool(name="raw", bufs=1))
        stream = ctx.enter_context(tc.tile_pool(name="stream", bufs=5))
        sorted_ = ctx.enter_context(tc.tile_pool(name="sorted", bufs=2))
        group = ctx.enter_context(tc.tile_pool(name="group", bufs=3))
        codes = ctx.enter_context(tc.tile_pool(name="codes", bufs=3))
        keep = ctx.enter_context(tc.tile_pool(name="keep", bufs=1))
        result = ctx.enter_context(tc.tile_pool(name="result", bufs=8))
        psum_t = ctx.enter_context(tc.psum_pool(name="psum_t", bufs=4))
        psum_acc = ctx.enter_context(tc.psum_pool(name="psum_acc", bufs=4))
        ctx.enter_context(tc.manual_schedule())

        ident = const.tile([P, P], F32)
        make_identity(nc, ident[:])

        y2_raw = raw.tile([P, B_TILES, E], BF16)
        w2_raw = raw.tile([P, Z_PASSES, PACK, E], BF16)
        wi_raw = raw.tile([P, Z_PASSES, PACK, E], BF16)
        first_raw = raw.tile([P, B_TILES, M], BF16)
        b2 = const.tile([P, Z_PASSES, PACK], BF16)
        bi = const.tile([P, Z_PASSES, PACK], BF16)
        bo = const.tile([P, V], BF16)

        y2_rows = y2.rearrange("(c r) k -> c r k", r=B_TILES)
        w2_rows = w_second.rearrange("(g c t) k -> c g t k", g=Z_PASSES, t=PACK)
        wi_rows = w_int.rearrange("(g c t) k -> c g t k", g=Z_PASSES, t=PACK)
        nc.sync.dma_start(out=y2_raw[:, 0:2, :], in_=y2_rows[:, 0:2, :])
        nc.sync.dma_start(out=y2_raw[:, 2:4, :], in_=y2_rows[:, 2:4, :])
        for g in range(Z_PASSES):
            nc.sync.dma_start(out=w2_raw[:, g, :, :], in_=w2_rows[:, g, :, :])
        for bias, vector in ((b2, b_second), (bi, b_int)):
            nc.sync.dma_start(
                out=bias[:], in_=vector.rearrange("(g c t) -> c g t", g=Z_PASSES, t=PACK)
            )
        for g in range(Z_PASSES):
            nc.sync.dma_start(out=wi_raw[:, g, :, :], in_=wi_rows[:, g, :, :])
        nc.sync.dma_start(
            out=first_raw[:], in_=first.rearrange("(c r) m -> c r m", r=B_TILES)
        )
        wo_raw = []

        def load_block(j):
            wo_raw.append(stream.tile([P, V_TILES, M], BF16, tag="wo_raw", name="wo_raw%d" % j))
            nc.sync.dma_start(
                out=wo_raw[j][:],
                in_=w_out[j * V_BLOCK : (j + 1) * V_BLOCK, :].rearrange(
                    "(s c) k -> c s k", s=V_TILES
                ),
            )

        for j in range(3):
            load_block(j)
        nc.sync.dma_start(out=bo[:], in_=b_out.partition_broadcast(P))
        for j in range(3, V_BLOCKS):
            load_block(j)

        on_scalar, on_vector = nc.scalar.copy, nc.vector.tensor_copy

        def turn(pieces, grouped, copy, sorted_words=False):
            bank = psum_t.tile([P, 2, 2, P], F32, tag="bank")
            for a in range(2):
                words = pieces[a].bitcast(F32)
                for u in range(2):
                    block = words[:, u * P : (u + 1) * P] if sorted_words else words[:, u : 2 * P : 2]
                    nc.tensor.transpose(bank[:, a, u, :], block, ident[:])
            copy(
                out=grouped.bitcast(F32).rearrange("p (a c u) -> p a c u", a=2, u=2),
                in_=bank[:].rearrange("p a u c -> p a c u"),
            )

        TURN = 2 * P * PACK

        def quantise(codes_, scales, grouped):
            nc.vector.quantize_mx(out=codes_.bitcast(FP8X4), scales=scales, in_=grouped)

        y2_g = keep.tile([P, B * PACK], BF16, align_bytes=64)
        w2_g = keep.tile([P, Z_PASSES, M * PACK // 2], BF16, align_bytes=64)
        wi_g = keep.tile([P, Z_PASSES, M * PACK // 2], BF16, align_bytes=64)
        z_g = keep.tile([P, Z_PASSES, B * PACK], BF16, align_bytes=64)
        y2_c = keep.tile([P, B], U32, align_bytes=64)
        y2_s = keep.tile([P, B], U8, align_bytes=64)
        w2_c = keep.tile([P, M], U32, align_bytes=64)
        w2_s = keep.tile([P, M], U8, align_bytes=64)
        wi_c = keep.tile([P, M], U32, align_bytes=64)
        wi_s = keep.tile([P, M], U8, align_bytes=64)
        z_c = keep.tile([P, Z_PASSES, B], U32, align_bytes=64)
        z_s = keep.tile([P, Z_PASSES, B], U8, align_bytes=64)
        second = keep.tile([P, CHUNKS, B], F32)
        inter = keep.tile([P, CHUNKS, B], F32)

        def turn_y2(i, copy):
            turn(
                [y2_raw[:, 2 * i, :], y2_raw[:, 2 * i + 1, :]],
                y2_g[:, i * TURN : (i + 1) * TURN],
                copy,
            )

        def turn_weight(w_raw, w_g, i, copy):
            g, h = i // 2, i % 2
            turn(
                [w_raw[:, g, 2 * h, :], w_raw[:, g, 2 * h + 1, :]],
                w_g[:, g, h * TURN : (h + 1) * TURN],
                copy,
            )

        def quantise_weight(w_g, w_c, w_s, g):
            cols = slice(g * M // 2, (g + 1) * M // 2)
            quantise(w_c[:, cols], w_s[:, cols], w_g[:, g, :])

        def hidden_layer(w_c, w_s, bias, chunk, dest):
            cols = slice(chunk * P, (chunk + 1) * P)
            acc = psum_acc.tile([P, B], F32, tag="acc")
            nc.tensor.matmul_mx(
                out=acc[:],
                lhsT=w_c[:, cols].bitcast(FP8X4),
                lhsT_scale=w_s[:, cols],
                rhs=y2_c[:].bitcast(FP8X4),
                rhs_scale=y2_s[:],
                start=True,
                stop=True,
            )
            g, t = chunk // PACK, chunk % PACK
            nc.scalar.activation(
                out=dest[:, chunk, :], in_=acc[:], func=RELU, bias=bias[:, g, t : t + 1]
            )

        def times_first(q):
            g, u = q // 2, q % 2
            first_t = psum_t.tile([P, B], F32, tag="bank")
            for r in range(B_TILES):
                nc.tensor.transpose(
                    first_t[:, r * P : (r + 1) * P],
                    first_raw[:, r, :].bitcast(F32)[:, 2 * P * g + u : 2 * P * (g + 1) : 2],
                    ident[:],
                )
            nc.vector.tensor_tensor(
                out=second[:, 2 * q : 2 * q + 2, :],
                in0=second[:, 2 * q : 2 * q + 2, :],
                in1=first_t[:].bitcast(BF16).rearrange("p (n e) -> p e n", e=2),
                op=MULT,
            )

        def add_inter(g):
            nc.vector.tensor_tensor(
                out=z_g[:, g, :].rearrange("p (n t) -> p n t", t=PACK),
                in0=second[:, PACK * g : PACK * (g + 1), :].rearrange("p t n -> p n t"),
                in1=inter[:, PACK * g : PACK * (g + 1), :].rearrange("p t n -> p n t"),
                op=ADD,
            )

        wo_g, wo_c, wo_s = [], [], []
        wo_sorted = {}

        def sort_words(j, s, copy):
            if s == 0:
                wo_sorted[j] = sorted_.tile(
                    [P, V_TILES, M], BF16, tag="wo_sorted", name="wo_sorted%d" % j
                )
            copy(
                out=wo_sorted[j][:, s, :].bitcast(F32).rearrange("p (g u w) -> p g u w", g=2, u=2),
                in_=wo_raw[j][:, s, :].bitcast(F32).rearrange("p (g w u) -> p g u w", g=2, u=2),
            )

        def turn_block(j, i, copy):
            if i == 0:
                wo_g.append(
                    group.tile(
                        [P, Z_PASSES, V_BLOCK * PACK],
                        BF16,
                        tag="wo_g",
                        align_bytes=64,
                        name="wo_g%d" % j,
                    )
                )
            g, h = i // 2, i % 2
            cols = slice(g * K_PASS, (g + 1) * K_PASS)
            source = wo_sorted.get(j, wo_raw[j])
            turn(
                [source[:, 2 * h, cols], source[:, 2 * h + 1, cols]],
                wo_g[j][:, g, h * TURN : (h + 1) * TURN],
                copy,
                j in wo_sorted,
            )

        def quantise_block(j):
            wo_c.append(
                codes.tile(
                    [P, Z_PASSES, V_BLOCK], U32, tag="wo_c", align_bytes=64, name="wo_c%d" % j
                )
            )
            wo_s.append(
                codes.tile(
                    [P, Z_PASSES, V_BLOCK], U8, tag="wo_s", align_bytes=64, name="wo_s%d" % j
                )
            )
            quantise(
                wo_c[j][:].rearrange("p g n -> p (g n)"),
                wo_s[j][:].rearrange("p g n -> p (g n)"),
                wo_g[j][:].rearrange("p g x -> p (g x)"),
            )

        out_rows = out.rearrange("(c r) v -> c r v", r=B_TILES)

        def output_tile(j, r):
            cols = slice(j * V_BLOCK, (j + 1) * V_BLOCK)
            rows = slice(r * P, (r + 1) * P)
            acc = psum_acc.tile([P, V_BLOCK], F32, tag="acc")
            for g in range(Z_PASSES):
                nc.tensor.matmul_mx(
                    out=acc[:],
                    lhsT=z_c[:, g, rows].bitcast(FP8X4),
                    lhsT_scale=z_s[:, g, rows],
                    rhs=wo_c[j][:, g, :].bitcast(FP8X4),
                    rhs_scale=wo_s[j][:, g, :],
                    start=(g == 0),
                    stop=(g == Z_PASSES - 1),
                )
            res = result.tile([P, V_BLOCK], F32)
            nc.vector.tensor_tensor(out=res[:], in0=acc[:], in1=bo[:, cols], op=ADD)
            nc.sync.dma_start(out=out_rows[:, r, cols], in_=res[:])

        turn_y2(0, on_scalar)
        turn_y2(1, on_vector)
        quantise(y2_c[:], y2_s[:], y2_g[:])
        turn_weight(w2_raw, w2_g, 0, on_scalar)
        turn_weight(w2_raw, w2_g, 1, on_vector)
        turn_weight(w2_raw, w2_g, 2, on_scalar)
        turn_weight(w2_raw, w2_g, 3, on_scalar)
        quantise_weight(w2_g, w2_c, w2_s, 0)
        quantise_weight(w2_g, w2_c, w2_s, 1)
        turn_weight(wi_raw, wi_g, 0, on_vector)
        turn_weight(wi_raw, wi_g, 1, on_scalar)
        for chunk in range(0, 4):
            hidden_layer(w2_c, w2_s, b2, chunk, second)
        turn_weight(wi_raw, wi_g, 2, on_vector)
        turn_weight(wi_raw, wi_g, 3, on_vector)
        quantise_weight(wi_g, wi_c, wi_s, 0)
        for chunk in range(4, 8):
            hidden_layer(w2_c, w2_s, b2, chunk, second)
        quantise_weight(wi_g, wi_c, wi_s, 1)
        times_first(0)
        times_first(1)
        for chunk in range(0, 4):
            hidden_layer(wi_c, wi_s, bi, chunk, inter)
        times_first(2)
        times_first(3)
        for chunk in range(4, 8):
            hidden_layer(wi_c, wi_s, bi, chunk, inter)
        add_inter(0)
        turn_block(0, 0, on_scalar)
        turn_block(0, 1, on_scalar)
        turn_block(0, 2, on_scalar)
        turn_block(0, 3, on_scalar)
        add_inter(1)
        quantise(z_c[:, 0, :], z_s[:, 0, :], z_g[:, 0, :])
        quantise_block(0)
        quantise(z_c[:, 1, :], z_s[:, 1, :], z_g[:, 1, :])
        turn_block(1, 0, on_scalar)
        turn_block(1, 1, on_scalar)
        turn_block(1, 2, on_scalar)
        turn_block(1, 3, on_scalar)
        quantise_block(1)
        turn_block(2, 0, on_scalar)
        turn_block(2, 1, on_scalar)
        turn_block(2, 2, on_scalar)
        turn_block(2, 3, on_scalar)
        for s in range(V_TILES):
            sort_words(3, s, on_scalar)
        for r in range(B_TILES):
            output_tile(0, r)
        quantise_block(2)
        turn_block(3, 0, on_scalar)
        turn_block(3, 1, on_scalar)
        turn_block(3, 2, on_scalar)
        turn_block(3, 3, on_vector)
        for s in range(V_TILES):
            sort_words(4, s, on_scalar)
        for r in range(B_TILES):
            output_tile(1, r)
        quantise_block(3)
        turn_block(4, 0, on_scalar)
        turn_block(4, 1, on_scalar)
        turn_block(4, 2, on_scalar)
        turn_block(4, 3, on_vector)
        for s in range(V_TILES):
            sort_words(5, s, on_scalar)
        for r in range(B_TILES):
            output_tile(2, r)
        quantise_block(4)
        turn_block(5, 0, on_scalar)
        turn_block(5, 1, on_scalar)
        turn_block(5, 2, on_scalar)
        turn_block(5, 3, on_vector)
        for s in range(V_TILES):
            sort_words(6, s, on_scalar)
        for r in range(B_TILES):
            output_tile(3, r)
        quantise_block(5)
        turn_block(6, 0, on_scalar)
        turn_block(6, 1, on_scalar)
        turn_block(6, 2, on_scalar)
        turn_block(6, 3, on_vector)
        for s in range(V_TILES):
            sort_words(7, s, on_scalar)
        for r in range(B_TILES):
            output_tile(4, r)
        quantise_block(6)
        turn_block(7, 0, on_scalar)
        turn_block(7, 1, on_scalar)
        turn_block(7, 2, on_scalar)
        turn_block(7, 3, on_vector)
        for r in range(B_TILES):
            output_tile(5, r)
        quantise_block(7)
        for r in range(B_TILES):
            output_tile(6, r)
        for r in range(B_TILES):
            output_tile(7, r)
